import numpy as np
import ml_dtypes


def mxq(x, axis, fmt="e4m3"):
    dtype, down = {"e4m3": (ml_dtypes.float8_e4m3fn, 7), "e5m2": (ml_dtypes.float8_e5m2, 14)}[fmt]
    v = np.moveaxis(np.asarray(x, np.float32).astype(ml_dtypes.bfloat16).astype(np.float64), axis, -1)
    blocks = v.reshape(v.shape[:-1] + (-1, 32))
    amax = np.abs(blocks).max(-1, keepdims=True)
    byte = np.maximum(np.where(amax > 0, np.frexp(amax)[1] - 1 + 127, 0) - down, 1)
    scale = np.exp2(byte - 127.0)
    codes = (blocks / scale).astype(np.float32).astype(dtype).astype(np.float64)
    return np.moveaxis((codes * scale).reshape(v.shape), -1, axis)


WIDE = False


def mx_kscale(k):
    if not WIDE:
        return np.ones(k)
    levels = np.array([10, -10, 5, -5, 0])
    a = np.random.permutation(np.resize(levels, k // 512 * 4)).reshape(k // 512, 4)
    idx = np.arange(k)
    return np.exp2(a[idx // 512, idx % 128 // 32])


BF16 = ml_dtypes.bfloat16


def bf(x):
    return np.asarray(x, np.float32).astype(BF16)


def f64(x):
    return np.asarray(x).astype(np.float64)


E2M1 = np.array([0.0, 0.5, 1.0, 1.5, 2.0, 3.0, 4.0, 6.0, -0.0, -0.5, -1.0, -1.5, -2.0, -3.0, -4.0, -6.0])


def pack_weight(w, fmt):
    k, n = w.shape
    w = f64(bf(w)).reshape(k // 32, 32, n)
    amax = np.abs(w).max(1)
    if fmt == "e4m3":
        byte = np.frexp(amax)[1] - 1 + 127 - 7
    else:
        mant, ex = np.frexp(amax / 6.0)
        byte = np.where(mant > 0.5, ex, ex - 1) + 127
    byte = np.clip(np.where(amax > 0, byte, 1), 1, 254)
    scaled = (w * np.exp2(127.0 - byte)[:, None, :]).reshape(k, n).astype(np.float32)
    by_word = np.ascontiguousarray(scaled.reshape(k // 512, 128, 4, n).transpose(0, 1, 3, 2))
    if fmt == "e4m3":
        words = by_word.astype(ml_dtypes.float8_e4m3fn).view(np.uint8)
    else:
        c = by_word.astype(ml_dtypes.float4_e2m1fn).view(np.uint8) & 0xF
        words = c[..., 0::2] | (c[..., 1::2] << 4)
    return np.ascontiguousarray(words), np.ascontiguousarray(byte.astype(np.uint8).reshape(k // 512, 16, n))


def unpack_weight(words, scales, fmt):
    g, p, n, _ = words.shape
    if fmt == "e4m3":
        vals = np.ascontiguousarray(words).view(ml_dtypes.float8_e4m3fn).astype(np.float64)
    else:
        nib = np.empty((g, p, n, 4), np.uint8)
        nib[..., 0::2] = words & 0xF
        nib[..., 1::2] = words >> 4
        vals = E2M1[nib]
    vals = vals * np.repeat(np.exp2(scales.astype(np.float64) - 127.0), 8, axis=1)[..., None]
    return vals.transpose(0, 1, 3, 2).reshape(g * 512, n)

def pack4(w):
    words, scales = pack_weight(w, "e2m1")
    return words.reshape(words.shape[0], 128, -1), scales


def unpack4(words, scales):
    return unpack_weight(words.reshape(words.shape[0], 128, -1, 2), scales, "e2m1")


B, HP, WP, E, F, NH, WS = 2, 32, 64, 1024, 2048, 16, 8
NWH, NWW = HP // WS, WP // WS
L, N = B * NWH * NWW, WS * WS
LN_EPS = 1e-5


def layernorm(x, g, b):
    mu = x.mean(-1, keepdims=True)
    var = ((x - mu) ** 2).mean(-1, keepdims=True)
    return (x - mu) / np.sqrt(var + LN_EPS) * g + b


def setup_inputs():
    s = mx_kscale(E)
    x = bf(np.random.standard_normal((B, HP * WP, E)))
    o = bf(np.random.standard_normal((L, N, E)) * 0.5 * s)
    out_w = np.random.standard_normal((E, E)) * 2.0 / np.sqrt(E) / s
    words, scales = pack4(np.ascontiguousarray(out_w.T))
    return {"x": x,
            "o": o,
            "out_w_words": words,
            "out_w_scales": scales,
            "out_b": bf(np.random.standard_normal(E) * 0.2),
            "ln1_g": bf(1.0 + 0.1 * np.random.standard_normal(E)),
            "ln1_b": bf(np.random.standard_normal(E) * 0.2)}


def reference(x, o, out_w_words, out_w_scales, out_b, ln1_g, ln1_b):
    xw = f64(x).reshape(B, NWH, WS, NWW, WS, E).transpose(0, 1, 3, 2, 4, 5).reshape(L, N, E)
    attn_out = (mxq(f64(o), 2, "e4m3") @ unpack4(out_w_words, out_w_scales)) + f64(out_b)
    return layernorm(xw + attn_out, f64(ln1_g), f64(ln1_b))

@@ -1,0 +1,256 @@
+from contextlib import ExitStack
+
+import concourse.mybir as mybir
+from concourse.masks import make_identity
+
+F32 = mybir.dt.float32
+BF16 = mybir.dt.bfloat16
+I32 = mybir.dt.int32
+U32 = mybir.dt.uint32
+U8 = mybir.dt.uint8
+FP8X4 = mybir.dt.float8_e4m3fn_x4
+FP4X4 = mybir.dt.float4_e2m1fn_x4
+ALU = mybir.AluOpType
+ACT = mybir.ActivationFunctionType
+
+P = 128
+E = 1024
+K_PASS = 512
+PASSES = E // K_PASS
+BANK = 512
+HALVES = E // BANK
+WINDOWS = 64
+WS = 8
+RUN = 4
+SLABS = WS
+BLOCKS = SLABS * RUN
+LN_EPS = 1e-5
+AHEAD = 2
+
+FLOPS = 2 * WINDOWS * WS * WS * E * E
+
+
+def tile_swintransformerblock_pa_t_kernel(
+    tc, x, o, out_w_words, out_w_scales, out_b, ln1_g, ln1_b, out
+):
+    nc = tc.nc
+
+    o_slabs = o.rearrange("l (r half j) e -> r l half (j e)", r=WS, half=2, j=RUN)
+    out_blocks = out.rearrange("l (r half j) e -> r j l half e", r=WS, half=2, j=RUN)
+    x_slabs = x.rearrange(
+        "b (wh r ww half j) e -> r (b wh) (ww half) (j e)", wh=4, r=WS, ww=8, half=2, j=RUN
+    )
+
+    with ExitStack() as stack:
+        stack.enter_context(tc.manual_schedule())
+        const = stack.enter_context(tc.tile_pool(name="const", bufs=1))
+        slabs = stack.enter_context(tc.tile_pool(name="slabs", bufs=AHEAD + 1))
+        work = stack.enter_context(tc.tile_pool(name="work", bufs=4))
+        stats = stack.enter_context(tc.tile_pool(name="stats", bufs=6))
+        psum_const = stack.enter_context(tc.psum_pool(name="psum_const", bufs=1))
+        psum_tr = stack.enter_context(tc.psum_pool(name="psum_tr", bufs=1))
+        psum_acc = stack.enter_context(tc.psum_pool(name="psum_acc", bufs=2))
+
+        o_tiles = {}
+        x_tiles = {}
+
+        def load_o(s):
+            o_tiles[s] = slabs.tile([P, RUN, E], BF16, name="o_slab")
+            nc.sync.dma_start(out=o_tiles[s][:].rearrange("p j e -> p (j e)"), in_=o_slabs[s])
+
+        def load_x(s):
+            x_tiles[s] = slabs.tile([P, RUN, E], BF16, name="x_slab")
+            nc.sync.dma_start(out=x_tiles[s][:].rearrange("p j e -> p (j e)"), in_=x_slabs[s])
+
+        w_scales = const.tile([P, PASSES, E], U8, align_bytes=64)
+        nc.vector.memset(w_scales[:].rearrange("p g n -> p (g n)").bitcast(I32), 0)
+        ones = const.tile([P, P], BF16)
+        nc.vector.memset(ones[:], 1.0)
+        vectors = const.tile([P, 3, E], BF16)
+        nc.vector.memset(vectors[:], 0.0)
+        eps = const.tile([P, 1], F32)
+        nc.vector.memset(eps[:], LN_EPS)
+        for v, vector in enumerate((ln1_g, ln1_b, out_b)):
+            nc.scalar.dma_start(out=vectors[0:1, v, :], in_=vector.unsqueeze(0))
+        identity = const.tile([P, P], F32)
+        make_identity(nc, identity[:])
+
+        load_o(0)
+        w_words = const.tile([P, PASSES, 2 * E], U8, align_bytes=64)
+        for g in range(PASSES):
+            nc.sync.dma_start(out=w_words[:, g, :].bitcast(I32), in_=out_w_words[g].bitcast(I32))
+        scale_rows = out_w_scales.bitcast(I32)
+        for quadrant in range(4):
+            nc.sync.dma_start(
+                out=w_scales[32 * quadrant : 32 * quadrant + 4].bitcast(I32),
+                in_=scale_rows[:, 4 * quadrant : 4 * quadrant + 4, :].rearrange("g q n -> q g n"),
+            )
+        load_x(0)
+        for s in range(1, AHEAD):
+            load_o(s)
+            load_x(s)
+
+        gain = psum_const.tile([P, E], F32)
+        shift_lo = psum_const.tile([P, BANK], F32)
+        shift_hi = const.tile([P, BANK], F32)
+        bias = const.tile([P, E], BF16)
+        for h in range(HALVES):
+            cols = slice(h * BANK, (h + 1) * BANK)
+            nc.tensor.matmul(gain[:, cols], lhsT=ones[:], rhs=vectors[:, 0, cols], start=True, stop=True)
+        nc.tensor.matmul(shift_lo[:], lhsT=ones[:], rhs=vectors[:, 1, 0:BANK], start=True, stop=True)
+        spread = psum_acc.tile([P, BANK], F32, name="acc0")
+        nc.tensor.matmul(spread[:], lhsT=ones[:], rhs=vectors[:, 1, BANK:E], start=True, stop=True)
+        nc.scalar.copy(out=shift_hi[:], in_=spread[:])
+        for h in range(HALVES):
+            cols = slice(h * BANK, (h + 1) * BANK)
+            spread = psum_acc.tile([P, BANK], F32, name="acc%d" % h)
+            nc.tensor.matmul(spread[:], lhsT=ones[:], rhs=vectors[:, 2, cols], start=True, stop=True)
+            nc.scalar.copy(out=bias[:, cols], in_=spread[:])
+
+        live = {}
+
+        def transpose_o(i):
+            o_words = o_tiles[i // RUN][:, i % RUN, :].bitcast(F32)
+            flipped = psum_tr.tile([P, PASSES, 2, P], F32, name="flipped")
+            for g in range(PASSES):
+                for u in range(2):
+                    nc.tensor.transpose(
+                        flipped[:, g, u, :], o_words[:, 256 * g + u : 256 * (g + 1) : 2], identity[:]
+                    )
+            grouped = work.tile([P, PASSES * P * 4], BF16, name="grouped", align_bytes=64)
+            nc.scalar.copy(
+                out=grouped[:].bitcast(F32).rearrange("p (g r u) -> p g r u", g=PASSES, u=2),
+                in_=flipped[:].rearrange("p g u r -> p g r u"),
+            )
+            live["grouped", i] = grouped
+
+        def add_bias(i):
+            x_bias = work.tile([P, E], F32, name="x_bias")
+            nc.gpsimd.tensor_tensor(
+                out=x_bias[:], in0=x_tiles[i // RUN][:, i % RUN, :], in1=bias[:], op=ALU.add
+            )
+            live["x_bias", i] = x_bias
+
+        def project(i):
+            codes = work.tile([P, PASSES * P], U32, name="codes", align_bytes=64)
+            scales = work.tile([P, PASSES * P], U8, name="scales", align_bytes=64)
+            nc.vector.quantize_mx(
+                out=codes[:].bitcast(FP8X4), scales=scales[:], in_=live["grouped", i][:]
+            )
+            for h in range(HALVES):
+                acc = psum_acc.tile([P, BANK], F32, name="acc%d" % h)
+                for g in range(PASSES):
+                    tokens = slice(g * P, (g + 1) * P)
+                    nc.tensor.matmul_mx(
+                        out=acc[:],
+                        lhsT=codes[:, tokens].bitcast(FP8X4),
+                        lhsT_scale=scales[:, tokens],
+                        rhs=w_words[:, g, 2 * h * BANK : 2 * (h + 1) * BANK].bitcast(FP4X4),
+                        rhs_scale=w_scales[:, g, h * BANK : (h + 1) * BANK],
+                        start=(g == 0),
+                        stop=(g == PASSES - 1),
+                    )
+                live["acc", i, h] = acc
+
+        def residual(i):
+            r = work.tile([P, E], F32, name="r")
+            row_sums = stats.tile([P, HALVES], F32, name="row_sums")
+            for h in range(HALVES):
+                cols = slice(h * BANK, (h + 1) * BANK)
+                nc.vector.scalar_tensor_tensor(
+                    out=r[:, cols],
+                    in0=live["acc", i, h][:],
+                    scalar=0.0,
+                    in1=live["x_bias", i][:, cols],
+                    op0=ALU.add,
+                    op1=ALU.add,
+                    accum_out=row_sums[:, h : h + 1],
+                )
+            live["r", i] = r
+            live["row_sums", i] = row_sums
+
+        def statistics(i):
+            neg_mean = stats.tile([P, 1], F32, name="neg_mean")
+            scaled_sums = stats.tile([P, HALVES], F32, name="scaled_sums")
+            nc.scalar.activation(
+                out=scaled_sums[:],
+                in_=live["row_sums", i][:],
+                func=ACT.Identity,
+                scale=-1.0 / E,
+                accum_out=neg_mean[:],
+            )
+            squares = work.tile([P, E], BF16, name="squares")
+            sum_squares = stats.tile([P, 1], F32, name="sum_squares")
+            nc.scalar.activation(
+                out=squares[:],
+                in_=live["r", i][:],
+                func=ACT.Square,
+                bias=neg_mean[:],
+                accum_out=sum_squares[:],
+            )
+            std = stats.tile([P, 1], F32, name="std")
+            nc.scalar.activation(
+                out=std[:], in_=sum_squares[:], func=ACT.Sqrt, bias=eps[:], scale=1.0 / E
+            )
+            live["neg_mean", i] = neg_mean
+            live["std", i] = std
+
+        def normalise(i):
+            rstd = stats.tile([P, 1], F32, name="rstd")
+            nc.vector.reciprocal(out=rstd[:], in_=live["std", i][:])
+            gained = work.tile([P, E], F32, name="gained")
+            for h in range(HALVES):
+                cols = slice(h * BANK, (h + 1) * BANK)
+                nc.vector.scalar_tensor_tensor(
+                    out=gained[:, cols],
+                    in0=live["r", i][:, cols],
+                    scalar=live["neg_mean", i][:],
+                    in1=gain[:, cols],
+                    op0=ALU.add,
+                    op1=ALU.mult,
+                )
+            result = work.tile([P, E], F32, name="result", bufs=6)
+            nc.vector.scalar_tensor_tensor(
+                out=result[:, 0:BANK],
+                in0=gained[:, 0:BANK],
+                scalar=rstd[:],
+                in1=shift_lo[:],
+                op0=ALU.mult,
+                op1=ALU.add,
+            )
+            live["rstd", i] = rstd
+            live["gained", i] = gained
+            live["result", i] = result
+
+        def scale_second_half(i):
+            scaled = work.tile([P, BANK], F32, name="scaled")
+            nc.scalar.activation(
+                out=scaled[:], in_=live["gained", i][:, BANK:E], func=ACT.Copy, scale=live["rstd", i][:]
+            )
+            live["scaled", i] = scaled
+
+        def shift_second_half_and_store(i):
+            result = live["result", i]
+            nc.gpsimd.tensor_tensor(
+                out=result[:, BANK:E], in0=live["scaled", i][:], in1=shift_hi[:], op=ALU.add
+            )
+            nc.sync.dma_start(out=out_blocks[i // RUN, i % RUN], in_=result[:])
+
+        stages = (
+            transpose_o,
+            project,
+            residual,
+            statistics,
+            normalise,
+            scale_second_half,
+            shift_second_half_and_store,
+        )
+        for k in range(BLOCKS + len(stages) - 1):
+            if k % RUN == 0 and k // RUN + AHEAD < SLABS:
+                load_o(k // RUN + AHEAD)
+                load_x(k // RUN + AHEAD)
+            if k < BLOCKS:
+                add_bias(k)
+            for lag, stage in enumerate(stages):
+                if 0 <= k - lag < BLOCKS:
+                    stage(k - lag)

@@ -25,7 +25,8 @@ RUN = 4
 SLABS = WS
 BLOCKS = SLABS * RUN
 LN_EPS = 1e-5
-AHEAD = 2
+GPSIMD_COLS = 256
+VECTOR_COLS = E - GPSIMD_COLS
 
 FLOPS = 2 * WINDOWS * WS * WS * E * E
 
@@ -44,12 +45,12 @@ def tile_swintransformerblock_pa_t_kernel(
     with ExitStack() as stack:
         stack.enter_context(tc.manual_schedule())
         const = stack.enter_context(tc.tile_pool(name="const", bufs=1))
-        slabs = stack.enter_context(tc.tile_pool(name="slabs", bufs=AHEAD + 1))
+        slabs = stack.enter_context(tc.tile_pool(name="slabs", bufs=2))
         work = stack.enter_context(tc.tile_pool(name="work", bufs=4))
         stats = stack.enter_context(tc.tile_pool(name="stats", bufs=6))
         psum_const = stack.enter_context(tc.psum_pool(name="psum_const", bufs=1))
         psum_tr = stack.enter_context(tc.psum_pool(name="psum_tr", bufs=1))
-        psum_acc = stack.enter_context(tc.psum_pool(name="psum_acc", bufs=2))
+        psum_acc = stack.enter_context(tc.psum_pool(name="psum_acc", bufs=3))
 
         o_tiles = {}
         x_tiles = {}
@@ -85,27 +86,21 @@ def tile_swintransformerblock_pa_t_kernel(
                 out=w_scales[32 * quadrant : 32 * quadrant + 4].bitcast(I32),
                 in_=scale_rows[:, 4 * quadrant : 4 * quadrant + 4, :].rearrange("g q n -> q g n"),
             )
-        load_x(0)
-        for s in range(1, AHEAD):
-            load_o(s)
-            load_x(s)
 
         gain = psum_const.tile([P, E], F32)
-        shift_lo = psum_const.tile([P, BANK], F32)
-        shift_hi = const.tile([P, BANK], F32)
+        shift = psum_const.tile([P, E], F32)
         bias = const.tile([P, E], BF16)
         for h in range(HALVES):
             cols = slice(h * BANK, (h + 1) * BANK)
             nc.tensor.matmul(gain[:, cols], lhsT=ones[:], rhs=vectors[:, 0, cols], start=True, stop=True)
-        nc.tensor.matmul(shift_lo[:], lhsT=ones[:], rhs=vectors[:, 1, 0:BANK], start=True, stop=True)
-        spread = psum_acc.tile([P, BANK], F32, name="acc0")
-        nc.tensor.matmul(spread[:], lhsT=ones[:], rhs=vectors[:, 1, BANK:E], start=True, stop=True)
-        nc.scalar.copy(out=shift_hi[:], in_=spread[:])
-        for h in range(HALVES):
-            cols = slice(h * BANK, (h + 1) * BANK)
-            spread = psum_acc.tile([P, BANK], F32, name="acc%d" % h)
+            nc.tensor.matmul(shift[:, cols], lhsT=ones[:], rhs=vectors[:, 1, cols], start=True, stop=True)
+            spread = psum_acc.tile([P, BANK], F32, name="acc")
             nc.tensor.matmul(spread[:], lhsT=ones[:], rhs=vectors[:, 2, cols], start=True, stop=True)
             nc.scalar.copy(out=bias[:, cols], in_=spread[:])
+        shift_tail = const.tile([P, GPSIMD_COLS], F32)
+        spread = psum_acc.tile([P, BANK], F32, name="acc")
+        nc.tensor.matmul(spread[:], lhsT=ones[:], rhs=vectors[:, 1, BANK:E], start=True, stop=True)
+        nc.scalar.copy(out=shift_tail[:], in_=spread[:, BANK - GPSIMD_COLS : BANK])
 
         live = {}
 
@@ -117,12 +112,16 @@ def tile_swintransformerblock_pa_t_kernel(
                     nc.tensor.transpose(
                         flipped[:, g, u, :], o_words[:, 256 * g + u : 256 * (g + 1) : 2], identity[:]
                     )
-            grouped = work.tile([P, PASSES * P * 4], BF16, name="grouped", align_bytes=64)
+            if i % RUN == 0:
+                live["grouped", i // RUN] = slabs.tile(
+                    [P, RUN, PASSES * P * 4], BF16, name="grouped", align_bytes=64
+                )
             nc.scalar.copy(
-                out=grouped[:].bitcast(F32).rearrange("p (g r u) -> p g r u", g=PASSES, u=2),
+                out=live["grouped", i // RUN][:, i % RUN, :]
+                .bitcast(F32)
+                .rearrange("p (g r u) -> p g r u", g=PASSES, u=2),
                 in_=flipped[:].rearrange("p g u r -> p g r u"),
             )
-            live["grouped", i] = grouped
 
         def add_bias(i):
             x_bias = work.tile([P, E], F32, name="x_bias")
@@ -131,20 +130,28 @@ def tile_swintransformerblock_pa_t_kernel(
             )
             live["x_bias", i] = x_bias
 
-        def project(i):
-            codes = work.tile([P, PASSES * P], U32, name="codes", align_bytes=64)
-            scales = work.tile([P, PASSES * P], U8, name="scales", align_bytes=64)
+        def quantise(s):
+            codes = slabs.tile([P, RUN, PASSES * P], U32, name="codes", align_bytes=64)
+            scales = slabs.tile([P, RUN, PASSES * P], U8, name="scales", align_bytes=64)
             nc.vector.quantize_mx(
-                out=codes[:].bitcast(FP8X4), scales=scales[:], in_=live["grouped", i][:]
+                out=codes[:].rearrange("p j c -> p (j c)").bitcast(FP8X4),
+                scales=scales[:].rearrange("p j c -> p (j c)"),
+                in_=live["grouped", s][:].rearrange("p j c -> p (j c)"),
             )
+            live["codes", s] = codes
+            live["scales", s] = scales
+
+        def project(i):
+            codes = live["codes", i // RUN]
+            scales = live["scales", i // RUN]
             for h in range(HALVES):
-                acc = psum_acc.tile([P, BANK], F32, name="acc%d" % h)
+                acc = psum_acc.tile([P, BANK], F32, name="acc")
                 for g in range(PASSES):
                     tokens = slice(g * P, (g + 1) * P)
                     nc.tensor.matmul_mx(
                         out=acc[:],
-                        lhsT=codes[:, tokens].bitcast(FP8X4),
-                        lhsT_scale=scales[:, tokens],
+                        lhsT=codes[:, i % RUN, tokens].bitcast(FP8X4),
+                        lhsT_scale=scales[:, i % RUN, tokens],
                         rhs=w_words[:, g, 2 * h * BANK : 2 * (h + 1) * BANK].bitcast(FP4X4),
                         rhs_scale=w_scales[:, g, h * BANK : (h + 1) * BANK],
                         start=(g == 0),
@@ -188,16 +195,18 @@ def tile_swintransformerblock_pa_t_kernel(
                 bias=neg_mean[:],
                 accum_out=sum_squares[:],
             )
-            std = stats.tile([P, 1], F32, name="std")
+            rstd = stats.tile([P, 1], F32, name="rstd")
             nc.scalar.activation(
-                out=std[:], in_=sum_squares[:], func=ACT.Sqrt, bias=eps[:], scale=1.0 / E
+                out=rstd[:],
+                in_=sum_squares[:],
+                func=ACT.Abs_reciprocal_sqrt,
+                bias=eps[:],
+                scale=1.0 / E,
             )
             live["neg_mean", i] = neg_mean
-            live["std", i] = std
+            live["rstd", i] = rstd
 
         def normalise(i):
-            rstd = stats.tile([P, 1], F32, name="rstd")
-            nc.vector.reciprocal(out=rstd[:], in_=live["std", i][:])
             gained = work.tile([P, E], F32, name="gained")
             for h in range(HALVES):
                 cols = slice(h * BANK, (h + 1) * BANK)
@@ -210,47 +219,53 @@ def tile_swintransformerblock_pa_t_kernel(
                     op1=ALU.mult,
                 )
             result = work.tile([P, E], F32, name="result", bufs=6)
-            nc.vector.scalar_tensor_tensor(
-                out=result[:, 0:BANK],
-                in0=gained[:, 0:BANK],
-                scalar=rstd[:],
-                in1=shift_lo[:],
-                op0=ALU.mult,
-                op1=ALU.add,
-            )
-            live["rstd", i] = rstd
+            for h in range(HALVES):
+                cols = slice(h * BANK, min((h + 1) * BANK, VECTOR_COLS))
+                nc.vector.scalar_tensor_tensor(
+                    out=result[:, cols],
+                    in0=gained[:, cols],
+                    scalar=live["rstd", i][:],
+                    in1=shift[:, cols],
+                    op0=ALU.mult,
+                    op1=ALU.add,
+                )
             live["gained", i] = gained
             live["result", i] = result
 
-        def scale_second_half(i):
-            scaled = work.tile([P, BANK], F32, name="scaled")
+        def scale_tail(i):
+            scaled = work.tile([P, GPSIMD_COLS], F32, name="scaled")
             nc.scalar.activation(
-                out=scaled[:], in_=live["gained", i][:, BANK:E], func=ACT.Copy, scale=live["rstd", i][:]
+                out=scaled[:],
+                in_=live["gained", i][:, VECTOR_COLS:E],
+                func=ACT.Copy,
+                scale=live["rstd", i][:],
             )
             live["scaled", i] = scaled
 
-        def shift_second_half_and_store(i):
+        def shift_tail_and_store(i):
             result = live["result", i]
             nc.gpsimd.tensor_tensor(
-                out=result[:, BANK:E], in0=live["scaled", i][:], in1=shift_hi[:], op=ALU.add
+                out=result[:, VECTOR_COLS:E], in0=live["scaled", i][:], in1=shift_tail[:], op=ALU.add
             )
             nc.sync.dma_start(out=out_blocks[i // RUN, i % RUN], in_=result[:])
 
-        stages = (
-            transpose_o,
-            project,
-            residual,
-            statistics,
-            normalise,
-            scale_second_half,
-            shift_second_half_and_store,
-        )
-        for k in range(BLOCKS + len(stages) - 1):
-            if k % RUN == 0 and k // RUN + AHEAD < SLABS:
-                load_o(k // RUN + AHEAD)
-                load_x(k // RUN + AHEAD)
-            if k < BLOCKS:
-                add_bias(k)
-            for lag, stage in enumerate(stages):
-                if 0 <= k - lag < BLOCKS:
-                    stage(k - lag)
+        def run(stage, i):
+            if 0 <= i < BLOCKS:
+                stage(i)
+
+        for k in range(BLOCKS + 11):
+            if k % RUN == 0:
+                if k // RUN + 1 < SLABS:
+                    load_o(k // RUN + 1)
+                if k // RUN < SLABS:
+                    load_x(k // RUN)
+            run(transpose_o, k)
+            if k % RUN == 0 and 0 < k <= BLOCKS:
+                quantise(k // RUN - 1)
+            run(add_bias, k - 4)
+            run(project, k - 5)
+            run(residual, k - 6)
+            run(statistics, k - 7)
+            run(normalise, k - 8)
+            run(scale_tail, k - 9)
+            run(shift_tail_and_store, k - 10)

@@ -19,16 +19,13 @@ K_PASS = 512
 PASSES = E // K_PASS
 BANK = 512
 HALVES = E // BANK
-WINDOWS = 64
 WS = 8
-RUN = 4
-SLABS = WS
-BLOCKS = SLABS * RUN
+TILES = 32
+GROUP = 4
+AHEAD = 4
 LN_EPS = 1e-5
-GPSIMD_COLS = 256
-VECTOR_COLS = E - GPSIMD_COLS
 
-FLOPS = 2 * WINDOWS * WS * WS * E * E
+FLOPS = 2 * TILES * P * E * E
 
 
 def tile_swintransformerblock_pa_t_kernel(
@@ -36,32 +33,32 @@ def tile_swintransformerblock_pa_t_kernel(
 ):
     nc = tc.nc
 
-    o_slabs = o.rearrange("l (r half j) e -> r l half (j e)", r=WS, half=2, j=RUN)
-    out_blocks = out.rearrange("l (r half j) e -> r j l half e", r=WS, half=2, j=RUN)
-    x_slabs = x.rearrange(
-        "b (wh r ww half j) e -> r (b wh) (ww half) (j e)", wh=4, r=WS, ww=8, half=2, j=RUN
+    o_tiles = o.rearrange("l (r half j) e -> r j l half e", r=WS, half=2, j=4)
+    out_tiles = out.rearrange("l (r half j) e -> r j l half e", r=WS, half=2, j=4)
+    x_tiles = x.rearrange(
+        "b (wh r ww half j) e -> r j (b wh) (ww half) e", wh=4, r=WS, ww=8, half=2, j=4
     )
 
     with ExitStack() as stack:
         stack.enter_context(tc.manual_schedule())
         const = stack.enter_context(tc.tile_pool(name="const", bufs=1))
-        slabs = stack.enter_context(tc.tile_pool(name="slabs", bufs=2))
+        loads = stack.enter_context(tc.tile_pool(name="loads", bufs=AHEAD + 2))
+        groups = stack.enter_context(tc.tile_pool(name="groups", bufs=2))
         work = stack.enter_context(tc.tile_pool(name="work", bufs=4))
         stats = stack.enter_context(tc.tile_pool(name="stats", bufs=6))
         psum_const = stack.enter_context(tc.psum_pool(name="psum_const", bufs=1))
-        psum_tr = stack.enter_context(tc.psum_pool(name="psum_tr", bufs=1))
+        psum_flip = stack.enter_context(tc.psum_pool(name="psum_flip", bufs=1))
         psum_acc = stack.enter_context(tc.psum_pool(name="psum_acc", bufs=3))
 
-        o_tiles = {}
-        x_tiles = {}
+        live = {}
 
-        def load_o(s):
-            o_tiles[s] = slabs.tile([P, RUN, E], BF16, name="o_slab")
-            nc.sync.dma_start(out=o_tiles[s][:].rearrange("p j e -> p (j e)"), in_=o_slabs[s])
+        def load_o(i):
+            live["o", i] = loads.tile([P, E], BF16, name="o_sb")
+            nc.sync.dma_start(out=live["o", i][:], in_=o_tiles[i // 4, i % 4])
 
-        def load_x(s):
-            x_tiles[s] = slabs.tile([P, RUN, E], BF16, name="x_slab")
-            nc.sync.dma_start(out=x_tiles[s][:].rearrange("p j e -> p (j e)"), in_=x_slabs[s])
+        def load_x(i):
+            live["x", i] = loads.tile([P, E], BF16, name="x_sb")
+            nc.sync.dma_start(out=live["x", i][:], in_=x_tiles[i // 4, i % 4])
 
         w_scales = const.tile([P, PASSES, E], U8, align_bytes=64)
         nc.vector.memset(w_scales[:].rearrange("p g n -> p (g n)").bitcast(I32), 0)
@@ -71,12 +68,13 @@ def tile_swintransformerblock_pa_t_kernel(
         nc.vector.memset(vectors[:], 0.0)
         eps = const.tile([P, 1], F32)
         nc.vector.memset(eps[:], LN_EPS)
-        for v, vector in enumerate((ln1_g, ln1_b, out_b)):
+        for v, vector in enumerate((ln1_g, out_b, ln1_b)):
             nc.scalar.dma_start(out=vectors[0:1, v, :], in_=vector.unsqueeze(0))
         identity = const.tile([P, P], F32)
         make_identity(nc, identity[:])
 
         load_o(0)
+        load_x(0)
         w_words = const.tile([P, PASSES, 2 * E], U8, align_bytes=64)
         for g in range(PASSES):
             nc.sync.dma_start(out=w_words[:, g, :].bitcast(I32), in_=out_w_words[g].bitcast(I32))
@@ -86,53 +84,43 @@ def tile_swintransformerblock_pa_t_kernel(
                 out=w_scales[32 * quadrant : 32 * quadrant + 4].bitcast(I32),
                 in_=scale_rows[:, 4 * quadrant : 4 * quadrant + 4, :].rearrange("g q n -> q g n"),
             )
+        for i in range(1, AHEAD):
+            load_o(i)
+            load_x(i)
 
         gain = psum_const.tile([P, E], F32)
-        shift = psum_const.tile([P, E], F32)
-        bias = const.tile([P, E], BF16)
+        bias = psum_const.tile([P, E], F32)
+        shift = const.tile([P, E], F32)
         for h in range(HALVES):
             cols = slice(h * BANK, (h + 1) * BANK)
             nc.tensor.matmul(gain[:, cols], lhsT=ones[:], rhs=vectors[:, 0, cols], start=True, stop=True)
-            nc.tensor.matmul(shift[:, cols], lhsT=ones[:], rhs=vectors[:, 1, cols], start=True, stop=True)
+            nc.tensor.matmul(bias[:, cols], lhsT=ones[:], rhs=vectors[:, 1, cols], start=True, stop=True)
             spread = psum_acc.tile([P, BANK], F32, name="acc")
             nc.tensor.matmul(spread[:], lhsT=ones[:], rhs=vectors[:, 2, cols], start=True, stop=True)
-            nc.scalar.copy(out=bias[:, cols], in_=spread[:])
-        shift_tail = const.tile([P, GPSIMD_COLS], F32)
-        spread = psum_acc.tile([P, BANK], F32, name="acc")
-        nc.tensor.matmul(spread[:], lhsT=ones[:], rhs=vectors[:, 1, BANK:E], start=True, stop=True)
-        nc.scalar.copy(out=shift_tail[:], in_=spread[:, BANK - GPSIMD_COLS : BANK])
-
-        live = {}
+            nc.scalar.copy(out=shift[:, cols], in_=spread[:])
 
         def transpose_o(i):
-            o_words = o_tiles[i // RUN][:, i % RUN, :].bitcast(F32)
-            flipped = psum_tr.tile([P, PASSES, 2, P], F32, name="flipped")
+            o_words = live["o", i][:].bitcast(F32)
+            flipped = psum_flip.tile([P, PASSES, 2, P], F32, name="flipped")
             for g in range(PASSES):
                 for u in range(2):
                     nc.tensor.transpose(
                         flipped[:, g, u, :], o_words[:, 256 * g + u : 256 * (g + 1) : 2], identity[:]
                     )
-            if i % RUN == 0:
-                live["grouped", i // RUN] = slabs.tile(
-                    [P, RUN, PASSES * P * 4], BF16, name="grouped", align_bytes=64
+            if i % GROUP == 0:
+                live["grouped", i // GROUP] = groups.tile(
+                    [P, GROUP, PASSES * P * 4], BF16, name="grouped", align_bytes=64
                 )
             nc.scalar.copy(
-                out=live["grouped", i // RUN][:, i % RUN, :]
+                out=live["grouped", i // GROUP][:, i % GROUP, :]
                 .bitcast(F32)
                 .rearrange("p (g r u) -> p g r u", g=PASSES, u=2),
                 in_=flipped[:].rearrange("p g u r -> p g r u"),
             )
 
-        def add_bias(i):
-            x_bias = work.tile([P, E], F32, name="x_bias")
-            nc.gpsimd.tensor_tensor(
-                out=x_bias[:], in0=x_tiles[i // RUN][:, i % RUN, :], in1=bias[:], op=ALU.add
-            )
-            live["x_bias", i] = x_bias
-
         def quantise(s):
-            codes = slabs.tile([P, RUN, PASSES * P], U32, name="codes", align_bytes=64)
-            scales = slabs.tile([P, RUN, PASSES * P], U8, name="scales", align_bytes=64)
+            codes = groups.tile([P, GROUP, PASSES * P], U32, name="codes", align_bytes=64)
+            scales = groups.tile([P, GROUP, PASSES * P], U8, name="scales", align_bytes=64)
             nc.vector.quantize_mx(
                 out=codes[:].rearrange("p j c -> p (j c)").bitcast(FP8X4),
                 scales=scales[:].rearrange("p j c -> p (j c)"),
@@ -141,17 +129,26 @@ def tile_swintransformerblock_pa_t_kernel(
             live["codes", s] = codes
             live["scales", s] = scales
 
+        def add_bias(i):
+            x_bias = work.tile([P, E], F32, name="x_bias", bufs=9)
+            for h in range(HALVES):
+                cols = slice(h * BANK, (h + 1) * BANK)
+                nc.vector.tensor_tensor(
+                    out=x_bias[:, cols], in0=live["x", i][:, cols], in1=bias[:, cols], op=ALU.add
+                )
+            live["x_bias", i] = x_bias
+
         def project(i):
-            codes = live["codes", i // RUN]
-            scales = live["scales", i // RUN]
+            codes = live["codes", i // GROUP]
+            scales = live["scales", i // GROUP]
             for h in range(HALVES):
                 acc = psum_acc.tile([P, BANK], F32, name="acc")
                 for g in range(PASSES):
                     tokens = slice(g * P, (g + 1) * P)
                     nc.tensor.matmul_mx(
                         out=acc[:],
-                        lhsT=codes[:, i % RUN, tokens].bitcast(FP8X4),
-                        lhsT_scale=scales[:, i % RUN, tokens],
+                        lhsT=codes[:, i % GROUP, tokens].bitcast(FP8X4),
+                        lhsT_scale=scales[:, i % GROUP, tokens],
                         rhs=w_words[:, g, 2 * h * BANK : 2 * (h + 1) * BANK].bitcast(FP4X4),
                         rhs_scale=w_scales[:, g, h * BANK : (h + 1) * BANK],
                         start=(g == 0),
@@ -206,7 +203,7 @@ def tile_swintransformerblock_pa_t_kernel(
             live["neg_mean", i] = neg_mean
             live["rstd", i] = rstd
 
-        def normalise(i):
+        def apply_gain(i):
             gained = work.tile([P, E], F32, name="gained")
             for h in range(HALVES):
                 cols = slice(h * BANK, (h + 1) * BANK)
@@ -218,54 +215,34 @@ def tile_swintransformerblock_pa_t_kernel(
                     op0=ALU.add,
                     op1=ALU.mult,
                 )
-            result = work.tile([P, E], F32, name="result", bufs=6)
-            for h in range(HALVES):
-                cols = slice(h * BANK, min((h + 1) * BANK, VECTOR_COLS))
-                nc.vector.scalar_tensor_tensor(
-                    out=result[:, cols],
-                    in0=gained[:, cols],
-                    scalar=live["rstd", i][:],
-                    in1=shift[:, cols],
-                    op0=ALU.mult,
-                    op1=ALU.add,
-                )
             live["gained", i] = gained
-            live["result", i] = result
 
-        def scale_tail(i):
-            scaled = work.tile([P, GPSIMD_COLS], F32, name="scaled")
+        def divide_by_std(i):
+            scaled = work.tile([P, E], F32, name="scaled")
             nc.scalar.activation(
-                out=scaled[:],
-                in_=live["gained", i][:, VECTOR_COLS:E],
-                func=ACT.Copy,
-                scale=live["rstd", i][:],
+                out=scaled[:], in_=live["gained", i][:], func=ACT.Copy, scale=live["rstd", i][:]
             )
             live["scaled", i] = scaled
 
-        def shift_tail_and_store(i):
-            result = live["result", i]
-            nc.gpsimd.tensor_tensor(
-                out=result[:, VECTOR_COLS:E], in0=live["scaled", i][:], in1=shift_tail[:], op=ALU.add
-            )
-            nc.sync.dma_start(out=out_blocks[i // RUN, i % RUN], in_=result[:])
+        def add_shift_and_store(i):
+            result = work.tile([P, E], F32, name="result")
+            nc.gpsimd.tensor_tensor(out=result[:], in0=live["scaled", i][:], in1=shift[:], op=ALU.add)
+            nc.sync.dma_start(out=out_tiles[i // 4, i % 4], in_=result[:])
 
         def run(stage, i):
-            if 0 <= i < BLOCKS:
+            if 0 <= i < TILES:
                 stage(i)
 
-        for k in range(BLOCKS + 11):
-            if k % RUN == 0:
-                if k // RUN + 1 < SLABS:
-                    load_o(k // RUN + 1)
-                if k // RUN < SLABS:
-                    load_x(k // RUN)
+        for k in range(TILES + 11):
+            run(load_o, k + AHEAD)
+            run(load_x, k + AHEAD)
             run(transpose_o, k)
-            if k % RUN == 0 and 0 < k <= BLOCKS:
-                quantise(k // RUN - 1)
-            run(add_bias, k - 4)
+            if k % GROUP == 0 and 0 < k <= TILES:
+                quantise(k // GROUP - 1)
+            run(add_bias, k)
             run(project, k - 5)
             run(residual, k - 6)
             run(statistics, k - 7)
-            run(normalise, k - 8)
-            run(scale_tail, k - 9)
-            run(shift_tail_and_store, k - 10)
+            run(apply_gain, k - 8)
+            run(divide_by_std, k - 9)
+            run(add_shift_and_store, k - 10)

@@ -23,6 +23,7 @@ WS = 8
 TILES = 32
 GROUP = 4
 AHEAD = 4
+TAIL = 2
 LN_EPS = 1e-5
 
 FLOPS = 2 * TILES * P * E * E
@@ -60,24 +61,29 @@ def tile_swintransformerblock_pa_t_kernel(
             live["x", i] = loads.tile([P, E], BF16, name="x_sb")
             nc.sync.dma_start(out=live["x", i][:], in_=x_tiles[i // 4, i % 4])
 
-        w_scales = const.tile([P, PASSES, E], U8, align_bytes=64)
-        nc.vector.memset(w_scales[:].rearrange("p g n -> p (g n)").bitcast(I32), 0)
+        bias_row = const.tile([P, E], BF16)
+        gain_row = const.tile([P, E], BF16)
+        shift_row = const.tile([P, E], BF16)
         ones = const.tile([P, P], BF16)
-        nc.vector.memset(ones[:], 1.0)
-        vectors = const.tile([P, 3, E], BF16)
-        nc.vector.memset(vectors[:], 0.0)
         eps = const.tile([P, 1], F32)
+        w_scales = const.tile([P, PASSES, E], U8, align_bytes=64)
+
+        load_x(0)
+        load_o(0)
+        nc.vector.memset(bias_row[:], 0.0)
+        nc.scalar.dma_start(out=bias_row[0:1, :], in_=out_b.unsqueeze(0))
         nc.vector.memset(eps[:], LN_EPS)
-        for v, vector in enumerate((ln1_g, out_b, ln1_b)):
-            nc.scalar.dma_start(out=vectors[0:1, v, :], in_=vector.unsqueeze(0))
+        warm = const.tile([P, 1], F32)
+        nc.scalar.activation(out=warm[:], in_=eps[:], func=ACT.Abs_reciprocal_sqrt)
+        nc.vector.memset(ones[:], 1.0)
+        nc.vector.memset(w_scales[:].rearrange("p g n -> p (g n)").bitcast(I32), 0)
+        nc.vector.memset(gain_row[:], 0.0)
+        nc.scalar.dma_start(out=gain_row[0:1, :], in_=ln1_g.unsqueeze(0))
+        nc.vector.memset(shift_row[:], 0.0)
+        nc.scalar.dma_start(out=shift_row[0:1, :], in_=ln1_b.unsqueeze(0))
         identity = const.tile([P, P], F32)
         make_identity(nc, identity[:])
 
-        load_o(0)
-        load_x(0)
-        w_words = const.tile([P, PASSES, 2 * E], U8, align_bytes=64)
-        for g in range(PASSES):
-            nc.sync.dma_start(out=w_words[:, g, :].bitcast(I32), in_=out_w_words[g].bitcast(I32))
         scale_rows = out_w_scales.bitcast(I32)
         for quadrant in range(4):
             nc.sync.dma_start(
@@ -87,17 +93,29 @@ def tile_swintransformerblock_pa_t_kernel(
         for i in range(1, AHEAD):
             load_o(i)
             load_x(i)
+        w_words = const.tile([P, PASSES, 2 * E], U8, align_bytes=64)
+        for g in range(PASSES):
+            nc.sync.dma_start(out=w_words[:, g, :].bitcast(I32), in_=out_w_words[g].bitcast(I32))
 
+        def spread(psum_tile, row_tile):
+            for h in range(HALVES):
+                cols = slice(h * BANK, (h + 1) * BANK)
+                nc.tensor.matmul(psum_tile[:, cols], lhsT=ones[:], rhs=row_tile[:, cols], start=True, stop=True)
+
+        bias = psum_const.tile([P, E], F32, name="added")
+        spread(bias, bias_row)
         gain = psum_const.tile([P, E], F32)
-        bias = psum_const.tile([P, E], F32)
+        spread(gain, gain_row)
         shift = const.tile([P, E], F32)
         for h in range(HALVES):
             cols = slice(h * BANK, (h + 1) * BANK)
-            nc.tensor.matmul(gain[:, cols], lhsT=ones[:], rhs=vectors[:, 0, cols], start=True, stop=True)
-            nc.tensor.matmul(bias[:, cols], lhsT=ones[:], rhs=vectors[:, 1, cols], start=True, stop=True)
-            spread = psum_acc.tile([P, BANK], F32, name="acc")
-            nc.tensor.matmul(spread[:], lhsT=ones[:], rhs=vectors[:, 2, cols], start=True, stop=True)
-            nc.scalar.copy(out=shift[:, cols], in_=spread[:])
+            spread_half = psum_acc.tile([P, BANK], F32, name="acc")
+            nc.tensor.matmul(spread_half[:], lhsT=ones[:], rhs=shift_row[:, cols], start=True, stop=True)
+            nc.scalar.copy(out=shift[:, cols], in_=spread_half[:])
+
+        def shift_into_psum():
+            live["shift_psum"] = psum_const.tile([P, E], F32, name="added")
+            spread(live["shift_psum"], shift_row)
 
         def transpose_o(i):
             o_words = live["o", i][:].bitcast(F32)
@@ -229,8 +247,22 @@ def tile_swintransformerblock_pa_t_kernel(
             nc.gpsimd.tensor_tensor(out=result[:], in0=live["scaled", i][:], in1=shift[:], op=ALU.add)
             nc.sync.dma_start(out=out_tiles[i // 4, i % 4], in_=result[:])
 
-        def run(stage, i):
-            if 0 <= i < TILES:
+        def finish_on_vector(i):
+            result = work.tile([P, E], F32, name="result")
+            for h in range(HALVES):
+                cols = slice(h * BANK, (h + 1) * BANK)
+                nc.vector.scalar_tensor_tensor(
+                    out=result[:, cols],
+                    in0=live["gained", i][:, cols],
+                    scalar=live["rstd", i][:],
+                    in1=live["shift_psum"][:, cols],
+                    op0=ALU.mult,
+                    op1=ALU.add,
+                )
+                nc.sync.dma_start(out=out_tiles[i // 4, i % 4][:, :, cols], in_=result[:, cols])
+
+        def run(stage, i, first=0, last=TILES):
+            if first <= i < last:
                 stage(i)
 
         for k in range(TILES + 11):
@@ -244,5 +276,8 @@ def tile_swintransformerblock_pa_t_kernel(
             run(residual, k - 6)
             run(statistics, k - 7)
             run(apply_gain, k - 8)
-            run(divide_by_std, k - 9)
-            run(add_shift_and_store, k - 10)
+            if k == TILES:
+                shift_into_psum()
+            run(finish_on_vector, k - 9, first=TILES - TAIL)
+            run(divide_by_std, k - 9, last=TILES - TAIL)
+            run(add_shift_and_store, k - 10, last=TILES - TAIL)

@@ -24,6 +24,7 @@ TILES = 32
 GROUP = 4
 AHEAD = 4
 TAIL = 2
+POOL_EVERY = 6
 LN_EPS = 1e-5
 
 FLOPS = 2 * TILES * P * E * E
@@ -71,31 +72,31 @@ def tile_swintransformerblock_pa_t_kernel(
         load_x(0)
         load_o(0)
         nc.vector.memset(bias_row[:], 0.0)
-        nc.scalar.dma_start(out=bias_row[0:1, :], in_=out_b.unsqueeze(0))
+        nc.sync.dma_start(out=bias_row[0:1, :], in_=out_b.unsqueeze(0))
         nc.vector.memset(eps[:], LN_EPS)
         warm = const.tile([P, 1], F32)
         nc.scalar.activation(out=warm[:], in_=eps[:], func=ACT.Abs_reciprocal_sqrt)
         nc.vector.memset(ones[:], 1.0)
         nc.vector.memset(w_scales[:].rearrange("p g n -> p (g n)").bitcast(I32), 0)
         nc.vector.memset(gain_row[:], 0.0)
-        nc.scalar.dma_start(out=gain_row[0:1, :], in_=ln1_g.unsqueeze(0))
         nc.vector.memset(shift_row[:], 0.0)
-        nc.scalar.dma_start(out=shift_row[0:1, :], in_=ln1_b.unsqueeze(0))
         identity = const.tile([P, P], F32)
         make_identity(nc, identity[:])
 
+        for i in range(1, AHEAD):
+            load_x(i)
+            load_o(i)
         scale_rows = out_w_scales.bitcast(I32)
         for quadrant in range(4):
             nc.sync.dma_start(
                 out=w_scales[32 * quadrant : 32 * quadrant + 4].bitcast(I32),
                 in_=scale_rows[:, 4 * quadrant : 4 * quadrant + 4, :].rearrange("g q n -> q g n"),
             )
-        for i in range(1, AHEAD):
-            load_o(i)
-            load_x(i)
         w_words = const.tile([P, PASSES, 2 * E], U8, align_bytes=64)
         for g in range(PASSES):
             nc.sync.dma_start(out=w_words[:, g, :].bitcast(I32), in_=out_w_words[g].bitcast(I32))
+        nc.sync.dma_start(out=gain_row[0:1, :], in_=ln1_g.unsqueeze(0))
+        nc.sync.dma_start(out=shift_row[0:1, :], in_=ln1_b.unsqueeze(0))
 
         def spread(psum_tile, row_tile):
             for h in range(HALVES):
@@ -105,13 +106,17 @@ def tile_swintransformerblock_pa_t_kernel(
         bias = psum_const.tile([P, E], F32, name="added")
         spread(bias, bias_row)
         gain = psum_const.tile([P, E], F32)
-        spread(gain, gain_row)
+        bias_sb = const.tile([P, E], F32)
         shift = const.tile([P, E], F32)
-        for h in range(HALVES):
-            cols = slice(h * BANK, (h + 1) * BANK)
-            spread_half = psum_acc.tile([P, BANK], F32, name="acc")
-            nc.tensor.matmul(spread_half[:], lhsT=ones[:], rhs=shift_row[:, cols], start=True, stop=True)
-            nc.scalar.copy(out=shift[:, cols], in_=spread_half[:])
+
+        def spread_gain_and_shift():
+            spread(gain, gain_row)
+            for sbuf_tile, row_tile in ((bias_sb, bias_row), (shift, shift_row)):
+                for h in range(HALVES):
+                    cols = slice(h * BANK, (h + 1) * BANK)
+                    spread_half = psum_acc.tile([P, BANK], F32, name="acc")
+                    nc.tensor.matmul(spread_half[:], lhsT=ones[:], rhs=row_tile[:, cols], start=True, stop=True)
+                    nc.scalar.copy(out=sbuf_tile[:, cols], in_=spread_half[:])
 
         def shift_into_psum():
             live["shift_psum"] = psum_const.tile([P, E], F32, name="added")
@@ -149,12 +154,15 @@ def tile_swintransformerblock_pa_t_kernel(
 
         def add_bias(i):
             x_bias = work.tile([P, E], F32, name="x_bias", bufs=9)
+            live["x_bias", i] = x_bias
+            if i % POOL_EVERY == POOL_EVERY - 1:
+                nc.gpsimd.tensor_tensor(out=x_bias[:], in0=live["x", i][:], in1=bias_sb[:], op=ALU.add)
+                return
             for h in range(HALVES):
                 cols = slice(h * BANK, (h + 1) * BANK)
                 nc.vector.tensor_tensor(
                     out=x_bias[:, cols], in0=live["x", i][:, cols], in1=bias[:, cols], op=ALU.add
                 )
-            live["x_bias", i] = x_bias
 
         def project(i):
             codes = live["codes", i // GROUP]
@@ -269,6 +277,8 @@ def tile_swintransformerblock_pa_t_kernel(
             run(load_o, k + AHEAD)
             run(load_x, k + AHEAD)
             run(transpose_o, k)
+            if k == GROUP:
+                spread_gain_and_shift()
             if k % GROUP == 0 and 0 < k <= TILES:
                 quantise(k // GROUP - 1)
             run(add_bias, k)

@@ -152,17 +152,16 @@ def tile_swintransformerblock_pa_t_kernel(
             live["codes", s] = codes
             live["scales", s] = scales
 
-        def add_bias(i):
-            x_bias = work.tile([P, E], F32, name="x_bias", bufs=9)
-            live["x_bias", i] = x_bias
+        def add_bias(i, h):
+            if h == 0:
+                live["x_bias", i] = work.tile([P, E], F32, name="x_bias", bufs=9)
+            x_bias = live["x_bias", i]
             if i % POOL_EVERY == POOL_EVERY - 1:
-                nc.gpsimd.tensor_tensor(out=x_bias[:], in0=live["x", i][:], in1=bias_sb[:], op=ALU.add)
+                if h == 0:
+                    nc.gpsimd.tensor_tensor(out=x_bias[:], in0=live["x", i][:], in1=bias_sb[:], op=ALU.add)
                 return
-            for h in range(HALVES):
-                cols = slice(h * BANK, (h + 1) * BANK)
-                nc.vector.tensor_tensor(
-                    out=x_bias[:, cols], in0=live["x", i][:, cols], in1=bias[:, cols], op=ALU.add
-                )
+            cols = slice(h * BANK, (h + 1) * BANK)
+            nc.vector.tensor_tensor(out=x_bias[:, cols], in0=live["x", i][:, cols], in1=bias[:, cols], op=ALU.add)
 
         def project(i):
             codes = live["codes", i // GROUP]
@@ -182,22 +181,20 @@ def tile_swintransformerblock_pa_t_kernel(
                     )
                 live["acc", i, h] = acc
 
-        def residual(i):
-            r = work.tile([P, E], F32, name="r")
-            row_sums = stats.tile([P, HALVES], F32, name="row_sums")
-            for h in range(HALVES):
-                cols = slice(h * BANK, (h + 1) * BANK)
-                nc.vector.scalar_tensor_tensor(
-                    out=r[:, cols],
-                    in0=live["acc", i, h][:],
-                    scalar=0.0,
-                    in1=live["x_bias", i][:, cols],
-                    op0=ALU.add,
-                    op1=ALU.add,
-                    accum_out=row_sums[:, h : h + 1],
-                )
-            live["r", i] = r
-            live["row_sums", i] = row_sums
+        def residual(i, h):
+            if h == 0:
+                live["r", i] = work.tile([P, E], F32, name="r")
+                live["row_sums", i] = stats.tile([P, HALVES], F32, name="row_sums")
+            cols = slice(h * BANK, (h + 1) * BANK)
+            nc.vector.scalar_tensor_tensor(
+                out=live["r", i][:, cols],
+                in0=live["acc", i, h][:],
+                scalar=0.0,
+                in1=live["x_bias", i][:, cols],
+                op0=ALU.add,
+                op1=ALU.add,
+                accum_out=live["row_sums", i][:, h : h + 1],
+            )
 
         def statistics(i):
             neg_mean = stats.tile([P, 1], F32, name="neg_mean")
@@ -229,19 +226,18 @@ def tile_swintransformerblock_pa_t_kernel(
             live["neg_mean", i] = neg_mean
             live["rstd", i] = rstd
 
-        def apply_gain(i):
-            gained = work.tile([P, E], F32, name="gained")
-            for h in range(HALVES):
-                cols = slice(h * BANK, (h + 1) * BANK)
-                nc.vector.scalar_tensor_tensor(
-                    out=gained[:, cols],
-                    in0=live["r", i][:, cols],
-                    scalar=live["neg_mean", i][:],
-                    in1=gain[:, cols],
-                    op0=ALU.add,
-                    op1=ALU.mult,
-                )
-            live["gained", i] = gained
+        def apply_gain(i, h):
+            if h == 0:
+                live["gained", i] = work.tile([P, E], F32, name="gained")
+            cols = slice(h * BANK, (h + 1) * BANK)
+            nc.vector.scalar_tensor_tensor(
+                out=live["gained", i][:, cols],
+                in0=live["r", i][:, cols],
+                scalar=live["neg_mean", i][:],
+                in1=gain[:, cols],
+                op0=ALU.add,
+                op1=ALU.mult,
+            )
 
         def divide_by_std(i):
             scaled = work.tile([P, E], F32, name="scaled")
@@ -273,6 +269,10 @@ def tile_swintransformerblock_pa_t_kernel(
             if first <= i < last:
                 stage(i)
 
+        def run_half(stage, i, h):
+            if 0 <= i < TILES:
+                stage(i, h)
+
         for k in range(TILES + 11):
             run(load_o, k + AHEAD)
             run(load_x, k + AHEAD)
@@ -281,11 +281,17 @@ def tile_swintransformerblock_pa_t_kernel(
                 spread_gain_and_shift()
             if k % GROUP == 0 and 0 < k <= TILES:
                 quantise(k // GROUP - 1)
-            run(add_bias, k)
             run(project, k - 5)
-            run(residual, k - 6)
+            early = k < 8
+            for h in range(HALVES):
+                if early:
+                    run_half(add_bias, k, h)
+            for h in range(HALVES):
+                run_half(residual, k - 6, h)
+                run_half(apply_gain, k - 8, h)
+                if not early:
+                    run_half(add_bias, k, h)
             run(statistics, k - 7)
-            run(apply_gain, k - 8)
             if k == TILES:
                 shift_into_psum()
             run(finish_on_vector, k - 9, first=TILES - TAIL)

from contextlib import ExitStack

import concourse.mybir as mybir
from concourse.masks import make_identity

F32 = mybir.dt.float32
BF16 = mybir.dt.bfloat16
I32 = mybir.dt.int32
U32 = mybir.dt.uint32
U8 = mybir.dt.uint8
FP8X4 = mybir.dt.float8_e4m3fn_x4
FP4X4 = mybir.dt.float4_e2m1fn_x4
ALU = mybir.AluOpType
ACT = mybir.ActivationFunctionType

P = 128
E = 1024
K_PASS = 512
PASSES = E // K_PASS
BANK = 512
HALVES = E // BANK
WS = 8
TILES = 32
GROUP = 4
AHEAD = 4
TAIL = 2
POOL_EVERY = 6
LN_EPS = 1e-5

FLOPS = 2 * TILES * P * E * E


def tile_swintransformerblock_pa_t_kernel(
    tc, x, o, out_w_words, out_w_scales, out_b, ln1_g, ln1_b, out
):
    nc = tc.nc

    o_tiles = o.rearrange("l (r half j) e -> r j l half e", r=WS, half=2, j=4)
    out_tiles = out.rearrange("l (r half j) e -> r j l half e", r=WS, half=2, j=4)
    x_tiles = x.rearrange(
        "b (wh r ww half j) e -> r j (b wh) (ww half) e", wh=4, r=WS, ww=8, half=2, j=4
    )

    with ExitStack() as stack:
        stack.enter_context(tc.manual_schedule())
        const = stack.enter_context(tc.tile_pool(name="const", bufs=1))
        loads = stack.enter_context(tc.tile_pool(name="loads", bufs=AHEAD + 2))
        groups = stack.enter_context(tc.tile_pool(name="groups", bufs=2))
        work = stack.enter_context(tc.tile_pool(name="work", bufs=4))
        stats = stack.enter_context(tc.tile_pool(name="stats", bufs=6))
        psum_const = stack.enter_context(tc.psum_pool(name="psum_const", bufs=1))
        psum_flip = stack.enter_context(tc.psum_pool(name="psum_flip", bufs=1))
        psum_acc = stack.enter_context(tc.psum_pool(name="psum_acc", bufs=3))

        live = {}

        def load_o(i):
            live["o", i] = loads.tile([P, E], BF16, name="o_sb")
            nc.sync.dma_start(out=live["o", i][:], in_=o_tiles[i // 4, i % 4])

        def load_x(i):
            live["x", i] = loads.tile([P, E], BF16, name="x_sb")
            nc.sync.dma_start(out=live["x", i][:], in_=x_tiles[i // 4, i % 4])

        bias_row = const.tile([P, E], BF16)
        gain_row = const.tile([P, E], BF16)
        shift_row = const.tile([P, E], BF16)
        ones = const.tile([P, P], BF16)
        eps = const.tile([P, 1], F32)
        w_scales = const.tile([P, PASSES, E], U8, align_bytes=64)

        load_x(0)
        load_o(0)
        nc.vector.memset(bias_row[:], 0.0)
        nc.sync.dma_start(out=bias_row[0:1, :], in_=out_b.unsqueeze(0))
        nc.vector.memset(eps[:], LN_EPS)
        warm = const.tile([P, 1], F32)
        nc.scalar.activation(out=warm[:], in_=eps[:], func=ACT.Abs_reciprocal_sqrt)
        nc.vector.memset(ones[:], 1.0)
        nc.vector.memset(w_scales[:].rearrange("p g n -> p (g n)").bitcast(I32), 0)
        nc.vector.memset(gain_row[:], 0.0)
        nc.vector.memset(shift_row[:], 0.0)
        identity = const.tile([P, P], F32)
        make_identity(nc, identity[:])

        for i in range(1, AHEAD):
            load_x(i)
            load_o(i)
        scale_rows = out_w_scales.bitcast(I32)
        for quadrant in range(4):
            nc.sync.dma_start(
                out=w_scales[32 * quadrant : 32 * quadrant + 4].bitcast(I32),
                in_=scale_rows[:, 4 * quadrant : 4 * quadrant + 4, :].rearrange("g q n -> q g n"),
            )
        w_words = const.tile([P, PASSES, 2 * E], U8, align_bytes=64)
        for g in range(PASSES):
            nc.sync.dma_start(out=w_words[:, g, :].bitcast(I32), in_=out_w_words[g].bitcast(I32))
        nc.sync.dma_start(out=gain_row[0:1, :], in_=ln1_g.unsqueeze(0))
        nc.sync.dma_start(out=shift_row[0:1, :], in_=ln1_b.unsqueeze(0))

        def spread(psum_tile, row_tile):
            for h in range(HALVES):
                cols = slice(h * BANK, (h + 1) * BANK)
                nc.tensor.matmul(psum_tile[:, cols], lhsT=ones[:], rhs=row_tile[:, cols], start=True, stop=True)

        bias = psum_const.tile([P, E], F32, name="added")
        spread(bias, bias_row)
        gain = psum_const.tile([P, E], F32)
        bias_sb = const.tile([P, E], F32)
        shift = const.tile([P, E], F32)

        def spread_gain_and_shift():
            spread(gain, gain_row)
            for sbuf_tile, row_tile in ((bias_sb, bias_row), (shift, shift_row)):
                for h in range(HALVES):
                    cols = slice(h * BANK, (h + 1) * BANK)
                    spread_half = psum_acc.tile([P, BANK], F32, name="acc")
                    nc.tensor.matmul(spread_half[:], lhsT=ones[:], rhs=row_tile[:, cols], start=True, stop=True)
                    nc.scalar.copy(out=sbuf_tile[:, cols], in_=spread_half[:])

        def shift_into_psum():
            live["shift_psum"] = psum_const.tile([P, E], F32, name="added")
            spread(live["shift_psum"], shift_row)

        def transpose_o(i):
            o_words = live["o", i][:].bitcast(F32)
            flipped = psum_flip.tile([P, PASSES, 2, P], F32, name="flipped")
            for g in range(PASSES):
                for u in range(2):
                    nc.tensor.transpose(
                        flipped[:, g, u, :], o_words[:, 256 * g + u : 256 * (g + 1) : 2], identity[:]
                    )
            if i % GROUP == 0:
                live["grouped", i // GROUP] = groups.tile(
                    [P, GROUP, PASSES * P * 4], BF16, name="grouped", align_bytes=64
                )
            nc.scalar.copy(
                out=live["grouped", i // GROUP][:, i % GROUP, :]
                .bitcast(F32)
                .rearrange("p (g r u) -> p g r u", g=PASSES, u=2),
                in_=flipped[:].rearrange("p g u r -> p g r u"),
            )

        def quantise(s):
            codes = groups.tile([P, GROUP, PASSES * P], U32, name="codes", align_bytes=64)
            scales = groups.tile([P, GROUP, PASSES * P], U8, name="scales", align_bytes=64)
            nc.vector.quantize_mx(
                out=codes[:].rearrange("p j c -> p (j c)").bitcast(FP8X4),
                scales=scales[:].rearrange("p j c -> p (j c)"),
                in_=live["grouped", s][:].rearrange("p j c -> p (j c)"),
            )
            live["codes", s] = codes
            live["scales", s] = scales

        def add_bias(i, h):
            if h == 0:
                live["x_bias", i] = work.tile([P, E], F32, name="x_bias", bufs=9)
            x_bias = live["x_bias", i]
            if i % POOL_EVERY == POOL_EVERY - 1:
                if h == 0:
                    nc.gpsimd.tensor_tensor(out=x_bias[:], in0=live["x", i][:], in1=bias_sb[:], op=ALU.add)
                return
            cols = slice(h * BANK, (h + 1) * BANK)
            nc.vector.tensor_tensor(out=x_bias[:, cols], in0=live["x", i][:, cols], in1=bias[:, cols], op=ALU.add)

        def project(i):
            codes = live["codes", i // GROUP]
            scales = live["scales", i // GROUP]
            for h in range(HALVES):
                acc = psum_acc.tile([P, BANK], F32, name="acc")
                for g in range(PASSES):
                    tokens = slice(g * P, (g + 1) * P)
                    nc.tensor.matmul_mx(
                        out=acc[:],
                        lhsT=codes[:, i % GROUP, tokens].bitcast(FP8X4),
                        lhsT_scale=scales[:, i % GROUP, tokens],
                        rhs=w_words[:, g, 2 * h * BANK : 2 * (h + 1) * BANK].bitcast(FP4X4),
                        rhs_scale=w_scales[:, g, h * BANK : (h + 1) * BANK],
                        start=(g == 0),
                        stop=(g == PASSES - 1),
                    )
                live["acc", i, h] = acc

        def residual(i, h):
            if h == 0:
                live["r", i] = work.tile([P, E], F32, name="r")
                live["row_sums", i] = stats.tile([P, HALVES], F32, name="row_sums")
            cols = slice(h * BANK, (h + 1) * BANK)
            nc.vector.scalar_tensor_tensor(
                out=live["r", i][:, cols],
                in0=live["acc", i, h][:],
                scalar=0.0,
                in1=live["x_bias", i][:, cols],
                op0=ALU.add,
                op1=ALU.add,
                accum_out=live["row_sums", i][:, h : h + 1],
            )

        def statistics(i):
            neg_mean = stats.tile([P, 1], F32, name="neg_mean")
            scaled_sums = stats.tile([P, HALVES], F32, name="scaled_sums")
            nc.scalar.activation(
                out=scaled_sums[:],
                in_=live["row_sums", i][:],
                func=ACT.Identity,
                scale=-1.0 / E,
                accum_out=neg_mean[:],
            )
            squares = work.tile([P, E], BF16, name="squares")
            sum_squares = stats.tile([P, 1], F32, name="sum_squares")
            nc.scalar.activation(
                out=squares[:],
                in_=live["r", i][:],
                func=ACT.Square,
                bias=neg_mean[:],
                accum_out=sum_squares[:],
            )
            rstd = stats.tile([P, 1], F32, name="rstd")
            nc.scalar.activation(
                out=rstd[:],
                in_=sum_squares[:],
                func=ACT.Abs_reciprocal_sqrt,
                bias=eps[:],
                scale=1.0 / E,
            )
            live["neg_mean", i] = neg_mean
            live["rstd", i] = rstd

        def apply_gain(i, h):
            if h == 0:
                live["gained", i] = work.tile([P, E], F32, name="gained")
            cols = slice(h * BANK, (h + 1) * BANK)
            nc.vector.scalar_tensor_tensor(
                out=live["gained", i][:, cols],
                in0=live["r", i][:, cols],
                scalar=live["neg_mean", i][:],
                in1=gain[:, cols],
                op0=ALU.add,
                op1=ALU.mult,
            )

        def divide_by_std(i):
            scaled = work.tile([P, E], F32, name="scaled")
            nc.scalar.activation(
                out=scaled[:], in_=live["gained", i][:], func=ACT.Copy, scale=live["rstd", i][:]
            )
            live["scaled", i] = scaled

        def add_shift_and_store(i):
            result = work.tile([P, E], F32, name="result")
            nc.gpsimd.tensor_tensor(out=result[:], in0=live["scaled", i][:], in1=shift[:], op=ALU.add)
            nc.sync.dma_start(out=out_tiles[i // 4, i % 4], in_=result[:])

        def finish_on_vector(i):
            result = work.tile([P, E], F32, name="result")
            for h in range(HALVES):
                cols = slice(h * BANK, (h + 1) * BANK)
                nc.vector.scalar_tensor_tensor(
                    out=result[:, cols],
                    in0=live["gained", i][:, cols],
                    scalar=live["rstd", i][:],
                    in1=live["shift_psum"][:, cols],
                    op0=ALU.mult,
                    op1=ALU.add,
                )
                nc.sync.dma_start(out=out_tiles[i // 4, i % 4][:, :, cols], in_=result[:, cols])

        def run(stage, i, first=0, last=TILES):
            if first <= i < last:
                stage(i)

        def run_half(stage, i, h):
            if 0 <= i < TILES:
                stage(i, h)

        for k in range(TILES + 11):
            run(load_o, k + AHEAD)
            run(load_x, k + AHEAD)
            run(transpose_o, k)
            if k == GROUP:
                spread_gain_and_shift()
            if k % GROUP == 0 and 0 < k <= TILES:
                quantise(k // GROUP - 1)
            run(project, k - 5)
            early = k < 8
            for h in range(HALVES):
                if early:
                    run_half(add_bias, k, h)
            for h in range(HALVES):
                run_half(residual, k - 6, h)
                run_half(apply_gain, k - 8, h)
                if not early:
                    run_half(add_bias, k, h)
            run(statistics, k - 7)
            if k == TILES:
                shift_into_psum()
            run(finish_on_vector, k - 9, first=TILES - TAIL)
            run(divide_by_std, k - 9, last=TILES - TAIL)
            run(add_shift_and_store, k - 10, last=TILES - TAIL)
